import numpy as np
import ml_dtypes

BF16 = ml_dtypes.bfloat16


def bf(x):
    return np.asarray(x, np.float32).astype(BF16)


def f32(x):
    return np.asarray(x, np.float32)


def f64(x):
    return np.asarray(x).astype(np.float64)


def striped(idx):
    return np.tile(idx.reshape(-1, 16).T, (8, 1))


S, D, M, N = 256, 128, 512, 64
EPS = 1e-5


def ln_rows(v):
    m = v.mean(axis=-1, keepdims=True)
    d = v - m
    return d / np.sqrt((d * d).mean(axis=-1, keepdims=True) + EPS)


def setup_inputs():
    return {"table": bf(np.random.standard_normal((S, D))), "h_init": f32(0.5 * np.random.standard_normal((D, 1))), "l_init": f32(0.5 * np.random.standard_normal((D, 1))), "w": bf(np.random.standard_normal((D, M)) / np.sqrt(D)), "offs": striped(np.random.permutation(np.tile(np.arange(S), 2))[:N])}


def reference(table, h_init, l_init, w, offs):
    idx = offs[:16].T.reshape(-1)
    a = ln_rows(f64(table))
    xi = ln_rows(f64(l_init)[:, 0] + (f64(h_init)[:, 0] + a))
    return np.maximum(f64(w).T @ xi[idx].T, 0.0)

@@ -1,0 +1,92 @@
+import concourse.mybir as mybir
+from concourse.masks import make_identity
+
+S, D, M, N = 256, 128, 512, 64
+P = 128
+BLOCKS = S // P
+HEADS = M // P
+EPS = 1e-5
+FLOPS = 2 * D * M * N
+
+BF16, F32, U16 = mybir.dt.bfloat16, mybir.dt.float32, mybir.dt.uint16
+ALU = mybir.AluOpType
+ACT = mybir.ActivationFunctionType
+
+
+def tile_bdhhrm_kernel(tc, table, h_init, l_init, w, offs, out):
+    nc = tc.nc
+    with (
+        tc.tile_pool(name="held", bufs=1) as held,
+        tc.psum_pool(name="psum", bufs=1) as psum,
+    ):
+        words = held.tile([P, BLOCKS, D], BF16, name="words")
+        nc.sync.dma_start(words[:], table.rearrange("(b p) d -> p b d", p=P))
+        offsets = held.tile([P, N // 16], U16, name="offsets")
+        nc.sync.dma_start(offsets[:], offs)
+        h_rows = held.tile([P, D], F32, name="h_rows")
+        nc.scalar.dma_start(h_rows[:], h_init.rearrange("d one -> (d one)").partition_broadcast(P))
+        l_rows = held.tile([P, D], F32, name="l_rows")
+        nc.scalar.dma_start(l_rows[:], l_init.rearrange("d one -> (d one)").partition_broadcast(P))
+        weights = held.tile([D, M], BF16, name="weights")
+        nc.gpsimd.dma_start(weights[:], w)
+
+        identity = held.tile([P, P], BF16, name="identity")
+        make_identity(nc, identity[:])
+        states = held.tile([P, D], F32, name="states")
+        nc.gpsimd.tensor_tensor(states[:], h_rows[:], l_rows[:], ALU.add)
+
+        stats_a = held.tile([P, BLOCKS, 6], F32, name="stats_a")
+        mean_var_a = held.tile([P, BLOCKS, 2], F32, name="mean_var_a")
+        rstd_a = held.tile([P, BLOCKS], F32, name="rstd_a")
+        summed = held.tile([P, BLOCKS, D], F32, name="summed")
+        for b in range(BLOCKS):
+            nc.vector.bn_stats(stats_a[:, b, :], words[:, b, :])
+            nc.vector.bn_aggr(mean_var_a[:, b, :], stats_a[:, b, :])
+        for b in range(BLOCKS):
+            nc.scalar.activation(
+                rstd_a[:, b : b + 1], mean_var_a[:, b, 1:2], ACT.Abs_reciprocal_sqrt, bias=EPS
+            )
+        for b in range(BLOCKS):
+            nc.vector.scalar_tensor_tensor(
+                summed[:, b, :], words[:, b, :], rstd_a[:, b : b + 1], states[:], ALU.mult, ALU.add
+            )
+
+        stats_x = held.tile([P, BLOCKS, 6], F32, name="stats_x")
+        mean_var_x = held.tile([P, BLOCKS, 2], F32, name="mean_var_x")
+        rstd_x = held.tile([P, BLOCKS], F32, name="rstd_x")
+        xi_rows = held.tile([P, BLOCKS, D], BF16, name="xi_rows")
+        for b in range(BLOCKS):
+            nc.vector.bn_stats(stats_x[:, b, :], summed[:, b, :])
+            nc.vector.bn_aggr(mean_var_x[:, b, :], stats_x[:, b, :])
+        for b in range(BLOCKS):
+            nc.scalar.activation(
+                rstd_x[:, b : b + 1], mean_var_x[:, b, 1:2], ACT.Abs_reciprocal_sqrt, bias=EPS
+            )
+        for b in range(BLOCKS):
+            nc.vector.tensor_scalar(
+                xi_rows[:, b, :],
+                summed[:, b, :],
+                mean_var_x[:, b, 0:1],
+                rstd_x[:, b : b + 1],
+                ALU.subtract,
+                ALU.mult,
+            )
+
+        xi_flipped = psum.tile([D, S], BF16, name="xi_flipped")
+        for b in range(BLOCKS):
+            nc.tensor.transpose(xi_flipped[:, b * P : (b + 1) * P], xi_rows[:, b, :], identity[:])
+        xi = held.tile([D, S], BF16, name="xi")
+        nc.vector.tensor_copy(xi[:], xi_flipped[:])
+
+        product = psum.tile([P, HEADS, N], F32, name="product")
+        for head in range(HEADS):
+            nc.tensor.matmul(
+                product[:, head, :],
+                weights[:, head * P : (head + 1) * P],
+                xi[:].indirect(offsets[:]),
+                start=True,
+                stop=True,
+            )
+        result = held.tile([P, HEADS, N], F32, name="result")
+        nc.vector.tensor_scalar_max(result[:], product[:], 0.0)
+        nc.sync.dma_start(out.rearrange("(head p) j -> p head j", p=P), result[:])

@@ -23,17 +23,19 @@ def tile_bdhhrm_kernel(tc, table, h_init, l_init, w, offs, out):
         nc.sync.dma_start(words[:], table.rearrange("(b p) d -> p b d", p=P))
         offsets = held.tile([P, N // 16], U16, name="offsets")
         nc.sync.dma_start(offsets[:], offs)
-        h_rows = held.tile([P, D], F32, name="h_rows")
-        nc.scalar.dma_start(h_rows[:], h_init.rearrange("d one -> (d one)").partition_broadcast(P))
-        l_rows = held.tile([P, D], F32, name="l_rows")
-        nc.scalar.dma_start(l_rows[:], l_init.rearrange("d one -> (d one)").partition_broadcast(P))
+        state_rows = held.tile([2, D], F32, name="state_rows")
+        nc.scalar.dma_start(state_rows[0:1, :], h_init.rearrange("d one -> one d"))
+        nc.scalar.dma_start(state_rows[1:2, :], l_init.rearrange("d one -> one d"))
         weights = held.tile([D, M], BF16, name="weights")
         nc.gpsimd.dma_start(weights[:], w)
 
         identity = held.tile([P, P], BF16, name="identity")
         make_identity(nc, identity[:])
-        states = held.tile([P, D], F32, name="states")
-        nc.gpsimd.tensor_tensor(states[:], h_rows[:], l_rows[:], ALU.add)
+
+        ones = held.tile([2, P], F32, name="ones")
+        nc.vector.memset(ones[:], 1.0)
+        states = psum.tile([P, D], F32, name="states")
+        nc.tensor.matmul(states[:], ones[:], state_rows[:], start=True, stop=True)
 
         stats_a = held.tile([P, BLOCKS, 6], F32, name="stats_a")
         mean_var_a = held.tile([P, BLOCKS, 2], F32, name="mean_var_a")

@@ -27,7 +27,7 @@ def tile_bdhhrm_kernel(tc, table, h_init, l_init, w, offs, out):
         nc.scalar.dma_start(state_rows[0:1, :], h_init.rearrange("d one -> one d"))
         nc.scalar.dma_start(state_rows[1:2, :], l_init.rearrange("d one -> one d"))
         weights = held.tile([D, M], BF16, name="weights")
-        nc.gpsimd.dma_start(weights[:], w)
+        nc.sync.dma_start(weights[:], w)
 
         identity = held.tile([P, P], BF16, name="identity")
         make_identity(nc, identity[:])
@@ -74,21 +74,23 @@ def tile_bdhhrm_kernel(tc, table, h_init, l_init, w, offs, out):
                 ALU.mult,
             )
 
-        xi_flipped = psum.tile([D, S], BF16, name="xi_flipped")
-        for b in range(BLOCKS):
-            nc.tensor.transpose(xi_flipped[:, b * P : (b + 1) * P], xi_rows[:, b, :], identity[:])
         xi = held.tile([D, S], BF16, name="xi")
-        nc.vector.tensor_copy(xi[:], xi_flipped[:])
+        for b in range(BLOCKS):
+            xi_flipped = psum.tile([D, P], BF16, name=f"xi_flipped{b}")
+            nc.tensor.transpose(xi_flipped[:], xi_rows[:, b, :], identity[:])
+            nc.vector.tensor_copy(xi[:, b * P : (b + 1) * P], xi_flipped[:])
 
-        product = psum.tile([P, HEADS, N], F32, name="product")
+        out_heads = out.rearrange("(head p) j -> head p j", p=P)
         for head in range(HEADS):
+            product = psum.tile([P, N], F32, name=f"product{head}")
             nc.tensor.matmul(
-                product[:, head, :],
+                product[:],
                 weights[:, head * P : (head + 1) * P],
                 xi[:].indirect(offsets[:]),
                 start=True,
                 stop=True,
             )
-        result = held.tile([P, HEADS, N], F32, name="result")
-        nc.vector.tensor_scalar_max(result[:], product[:], 0.0)
-        nc.sync.dma_start(out.rearrange("(head p) j -> p head j", p=P), result[:])
+            result = held.tile([P, N], F32, name=f"result{head}")
+            nc.vector.tensor_scalar_max(result[:], product[:], 0.0)
+            queue = nc.sync if head % 2 == 0 else nc.scalar
+            queue.dma_start(out_heads[head], result[:])

@@ -4,7 +4,7 @@ from concourse.masks import make_identity
 S, D, M, N = 256, 128, 512, 64
 P = 128
 BLOCKS = S // P
-HEADS = M // P
+TURNS = M // P
 EPS = 1e-5
 FLOPS = 2 * D * M * N
 
@@ -27,10 +27,13 @@ def tile_bdhhrm_kernel(tc, table, h_init, l_init, w, offs, out):
         nc.scalar.dma_start(state_rows[0:1, :], h_init.rearrange("d one -> one d"))
         nc.scalar.dma_start(state_rows[1:2, :], l_init.rearrange("d one -> one d"))
         weights = held.tile([D, M], BF16, name="weights")
-        nc.sync.dma_start(weights[:], w)
+        nc.gpsimd.dma_start(weights[:], w)
 
         identity = held.tile([P, P], BF16, name="identity")
         make_identity(nc, identity[:])
+
+        w_turns = held.tile([D, TURNS, P], BF16, name="w_turns")
+        nc.gpsimd.tensor_copy(w_turns[:], weights[:].rearrange("d (p k) -> d k p", k=TURNS))
 
         ones = held.tile([2, P], F32, name="ones")
         nc.vector.memset(ones[:], 1.0)
@@ -74,23 +77,21 @@ def tile_bdhhrm_kernel(tc, table, h_init, l_init, w, offs, out):
                 ALU.mult,
             )
 
-        xi = held.tile([D, S], BF16, name="xi")
+        xi_flipped = psum.tile([D, S], BF16, name="xi_flipped")
         for b in range(BLOCKS):
-            xi_flipped = psum.tile([D, P], BF16, name=f"xi_flipped{b}")
-            nc.tensor.transpose(xi_flipped[:], xi_rows[:, b, :], identity[:])
-            nc.vector.tensor_copy(xi[:, b * P : (b + 1) * P], xi_flipped[:])
+            nc.tensor.transpose(xi_flipped[:, b * P : (b + 1) * P], xi_rows[:, b, :], identity[:])
+        xi = held.tile([D, S], BF16, name="xi")
+        nc.vector.tensor_copy(xi[:], xi_flipped[:])
 
-        out_heads = out.rearrange("(head p) j -> head p j", p=P)
-        for head in range(HEADS):
-            product = psum.tile([P, N], F32, name=f"product{head}")
+        product = psum.tile([P, TURNS, N], F32, name="product")
+        for k in range(TURNS):
             nc.tensor.matmul(
-                product[:],
-                weights[:, head * P : (head + 1) * P],
+                product[:, k, :],
+                w_turns[:, k, :],
                 xi[:].indirect(offsets[:]),
                 start=True,
                 stop=True,
             )
-            result = held.tile([P, N], F32, name=f"result{head}")
-            nc.vector.tensor_scalar_max(result[:], product[:], 0.0)
-            queue = nc.sync if head % 2 == 0 else nc.scalar
-            queue.dma_start(out_heads[head], result[:])
+        result = held.tile([P, TURNS, N], F32, name="result")
+        nc.vector.tensor_scalar_max(result[:], product[:], 0.0)
+        nc.sync.dma_start(out.rearrange("(p k) j -> p k j", k=TURNS), result[:])

@@ -4,7 +4,7 @@ from concourse.masks import make_identity
 S, D, M, N = 256, 128, 512, 64
 P = 128
 BLOCKS = S // P
-TURNS = M // P
+HEADS = M // P
 EPS = 1e-5
 FLOPS = 2 * D * M * N
 
@@ -32,46 +32,41 @@ def tile_bdhhrm_kernel(tc, table, h_init, l_init, w, offs, out):
         identity = held.tile([P, P], BF16, name="identity")
         make_identity(nc, identity[:])
 
-        w_turns = held.tile([D, TURNS, P], BF16, name="w_turns")
-        nc.gpsimd.tensor_copy(w_turns[:], weights[:].rearrange("d (p k) -> d k p", k=TURNS))
-
         ones = held.tile([2, P], F32, name="ones")
         nc.vector.memset(ones[:], 1.0)
         states = psum.tile([P, D], F32, name="states")
         nc.tensor.matmul(states[:], ones[:], state_rows[:], start=True, stop=True)
 
-        stats_a = held.tile([P, BLOCKS, 6], F32, name="stats_a")
-        mean_var_a = held.tile([P, BLOCKS, 2], F32, name="mean_var_a")
+        MEAN, SQUARES = 1, 2
+
+        stats_a = held.tile([P, BLOCKS, 3], F32, name="stats_a")
+        nc.vector.bn_stats(
+            stats_a[:].rearrange("p b k -> p (b k)"), words[:].rearrange("p b d -> p d b")
+        )
         rstd_a = held.tile([P, BLOCKS], F32, name="rstd_a")
+        nc.scalar.activation(
+            rstd_a[:], stats_a[:, :, SQUARES], ACT.Abs_reciprocal_sqrt, bias=EPS, scale=1.0 / D
+        )
         summed = held.tile([P, BLOCKS, D], F32, name="summed")
-        for b in range(BLOCKS):
-            nc.vector.bn_stats(stats_a[:, b, :], words[:, b, :])
-            nc.vector.bn_aggr(mean_var_a[:, b, :], stats_a[:, b, :])
-        for b in range(BLOCKS):
-            nc.scalar.activation(
-                rstd_a[:, b : b + 1], mean_var_a[:, b, 1:2], ACT.Abs_reciprocal_sqrt, bias=EPS
-            )
         for b in range(BLOCKS):
             nc.vector.scalar_tensor_tensor(
                 summed[:, b, :], words[:, b, :], rstd_a[:, b : b + 1], states[:], ALU.mult, ALU.add
             )
 
-        stats_x = held.tile([P, BLOCKS, 6], F32, name="stats_x")
-        mean_var_x = held.tile([P, BLOCKS, 2], F32, name="mean_var_x")
+        stats_x = held.tile([P, BLOCKS, 3], F32, name="stats_x")
+        nc.vector.bn_stats(
+            stats_x[:].rearrange("p b k -> p (b k)"), summed[:].rearrange("p b d -> p d b")
+        )
         rstd_x = held.tile([P, BLOCKS], F32, name="rstd_x")
+        nc.scalar.activation(
+            rstd_x[:], stats_x[:, :, SQUARES], ACT.Abs_reciprocal_sqrt, bias=EPS, scale=1.0 / D
+        )
         xi_rows = held.tile([P, BLOCKS, D], BF16, name="xi_rows")
-        for b in range(BLOCKS):
-            nc.vector.bn_stats(stats_x[:, b, :], summed[:, b, :])
-            nc.vector.bn_aggr(mean_var_x[:, b, :], stats_x[:, b, :])
-        for b in range(BLOCKS):
-            nc.scalar.activation(
-                rstd_x[:, b : b + 1], mean_var_x[:, b, 1:2], ACT.Abs_reciprocal_sqrt, bias=EPS
-            )
         for b in range(BLOCKS):
             nc.vector.tensor_scalar(
                 xi_rows[:, b, :],
                 summed[:, b, :],
-                mean_var_x[:, b, 0:1],
+                stats_x[:, b, MEAN : MEAN + 1],
                 rstd_x[:, b : b + 1],
                 ALU.subtract,
                 ALU.mult,
@@ -83,15 +78,15 @@ def tile_bdhhrm_kernel(tc, table, h_init, l_init, w, offs, out):
         xi = held.tile([D, S], BF16, name="xi")
         nc.vector.tensor_copy(xi[:], xi_flipped[:])
 
-        product = psum.tile([P, TURNS, N], F32, name="product")
-        for k in range(TURNS):
+        product = psum.tile([P, HEADS, N], F32, name="product")
+        for head in range(HEADS):
             nc.tensor.matmul(
-                product[:, k, :],
-                w_turns[:, k, :],
+                product[:, head, :],
+                weights[:, head * P : (head + 1) * P],
                 xi[:].indirect(offsets[:]),
                 start=True,
                 stop=True,
             )
-        result = held.tile([P, TURNS, N], F32, name="result")
+        result = held.tile([P, HEADS, N], F32, name="result")
         nc.vector.tensor_scalar_max(result[:], product[:], 0.0)
-        nc.sync.dma_start(out.rearrange("(p k) j -> p k j", k=TURNS), result[:])
+        nc.sync.dma_start(out.rearrange("(head p) j -> p head j", p=P), result[:])

@@ -19,13 +19,13 @@ def tile_bdhhrm_kernel(tc, table, h_init, l_init, w, offs, out):
         tc.tile_pool(name="held", bufs=1) as held,
         tc.psum_pool(name="psum", bufs=1) as psum,
     ):
+        state_rows = held.tile([2, D], F32, name="state_rows")
+        nc.sync.dma_start(state_rows[0:1, :], h_init.rearrange("d one -> one d"))
+        nc.scalar.dma_start(state_rows[1:2, :], l_init.rearrange("d one -> one d"))
         words = held.tile([P, BLOCKS, D], BF16, name="words")
         nc.sync.dma_start(words[:], table.rearrange("(b p) d -> p b d", p=P))
         offsets = held.tile([P, N // 16], U16, name="offsets")
         nc.sync.dma_start(offsets[:], offs)
-        state_rows = held.tile([2, D], F32, name="state_rows")
-        nc.scalar.dma_start(state_rows[0:1, :], h_init.rearrange("d one -> one d"))
-        nc.scalar.dma_start(state_rows[1:2, :], l_init.rearrange("d one -> one d"))
         weights = held.tile([D, M], BF16, name="weights")
         nc.gpsimd.dma_start(weights[:], w)
 

@@ -37,6 +37,12 @@ def tile_bdhhrm_kernel(tc, table, h_init, l_init, w, offs, out):
         states = psum.tile([P, D], F32, name="states")
         nc.tensor.matmul(states[:], ones[:], state_rows[:], start=True, stop=True)
 
+        scratch = psum.tile([P, S], F32, name="scratch")
+        for turn in range(6):
+            nc.tensor.matmul(
+                scratch[:], words[:, 0, :], words[:].rearrange("p b d -> p (b d)"), start=True, stop=True
+            )
+
         MEAN, SQUARES = 1, 2
 
         stats_a = held.tile([P, BLOCKS, 3], F32, name="stats_a")

@@ -84,15 +84,19 @@ def tile_bdhhrm_kernel(tc, table, h_init, l_init, w, offs, out):
         xi = held.tile([D, S], BF16, name="xi")
         nc.vector.tensor_copy(xi[:], xi_flipped[:])
 
-        product = psum.tile([P, HEADS, N], F32, name="product")
-        for head in range(HEADS):
-            nc.tensor.matmul(
-                product[:, head, :],
-                weights[:, head * P : (head + 1) * P],
-                xi[:].indirect(offsets[:]),
-                start=True,
-                stop=True,
-            )
-        result = held.tile([P, HEADS, N], F32, name="result")
-        nc.vector.tensor_scalar_max(result[:], product[:], 0.0)
-        nc.sync.dma_start(out.rearrange("(head p) j -> p head j", p=P), result[:])
+        PAIR = 2
+        out_pairs = out.rearrange("(pair head p) j -> pair p head j", head=PAIR, p=P)
+        for pair, queue in enumerate((nc.sync, nc.scalar)):
+            product = psum.tile([P, PAIR, N], F32, name=f"product{pair}")
+            for head in range(PAIR):
+                first = (pair * PAIR + head) * P
+                nc.tensor.matmul(
+                    product[:, head, :],
+                    weights[:, first : first + P],
+                    xi[:].indirect(offsets[:]),
+                    start=True,
+                    stop=True,
+                )
+            result = held.tile([P, PAIR, N], F32, name=f"result{pair}")
+            nc.vector.tensor_scalar_max(result[:], product[:], 0.0)
+            queue.dma_start(out_pairs[pair], result[:])

@@ -86,7 +86,7 @@ def tile_bdhhrm_kernel(tc, table, h_init, l_init, w, offs, out):
 
         PAIR = 2
         out_pairs = out.rearrange("(pair head p) j -> pair p head j", head=PAIR, p=P)
-        for pair, queue in enumerate((nc.sync, nc.scalar)):
+        for pair in range(HEADS // PAIR):
             product = psum.tile([P, PAIR, N], F32, name=f"product{pair}")
             for head in range(PAIR):
                 first = (pair * PAIR + head) * P
@@ -99,4 +99,4 @@ def tile_bdhhrm_kernel(tc, table, h_init, l_init, w, offs, out):
                 )
             result = held.tile([P, PAIR, N], F32, name=f"result{pair}")
             nc.vector.tensor_scalar_max(result[:], product[:], 0.0)
-            queue.dma_start(out_pairs[pair], result[:])
+            nc.sync.dma_start(out_pairs[pair], result[:])

@@ -84,19 +84,15 @@ def tile_bdhhrm_kernel(tc, table, h_init, l_init, w, offs, out):
         xi = held.tile([D, S], BF16, name="xi")
         nc.vector.tensor_copy(xi[:], xi_flipped[:])
 
-        PAIR = 2
-        out_pairs = out.rearrange("(pair head p) j -> pair p head j", head=PAIR, p=P)
-        for pair in range(HEADS // PAIR):
-            product = psum.tile([P, PAIR, N], F32, name=f"product{pair}")
-            for head in range(PAIR):
-                first = (pair * PAIR + head) * P
-                nc.tensor.matmul(
-                    product[:, head, :],
-                    weights[:, first : first + P],
-                    xi[:].indirect(offsets[:]),
-                    start=True,
-                    stop=True,
-                )
-            result = held.tile([P, PAIR, N], F32, name=f"result{pair}")
+        for head in range(HEADS):
+            product = psum.tile([P, N], F32, name=f"product{head}")
+            nc.tensor.matmul(
+                product[:],
+                weights[:, head * P : (head + 1) * P],
+                xi[:].indirect(offsets[:]),
+                start=True,
+                stop=True,
+            )
+            result = held.tile([P, N], F32, name=f"result{head}")
             nc.vector.tensor_scalar_max(result[:], product[:], 0.0)
-            nc.sync.dma_start(out_pairs[pair], result[:])
+            nc.sync.dma_start(out[head * P : (head + 1) * P, :], result[:])

@@ -38,7 +38,7 @@ def tile_bdhhrm_kernel(tc, table, h_init, l_init, w, offs, out):
         nc.tensor.matmul(states[:], ones[:], state_rows[:], start=True, stop=True)
 
         scratch = psum.tile([P, S], F32, name="scratch")
-        for turn in range(6):
+        for turn in range(8):
             nc.tensor.matmul(
                 scratch[:], words[:, 0, :], words[:].rearrange("p b d -> p (b d)"), start=True, stop=True
             )
@@ -78,11 +78,11 @@ def tile_bdhhrm_kernel(tc, table, h_init, l_init, w, offs, out):
                 ALU.mult,
             )
 
-        xi_flipped = psum.tile([D, S], BF16, name="xi_flipped")
-        for b in range(BLOCKS):
-            nc.tensor.transpose(xi_flipped[:, b * P : (b + 1) * P], xi_rows[:, b, :], identity[:])
         xi = held.tile([D, S], BF16, name="xi")
-        nc.vector.tensor_copy(xi[:], xi_flipped[:])
+        for b in range(BLOCKS):
+            flipped = psum.tile([D, P], BF16, name=f"flipped{b}")
+            nc.tensor.transpose(flipped[:], xi_rows[:, b, :], identity[:])
+            nc.vector.tensor_copy(xi[:, b * P : (b + 1) * P], flipped[:])
 
         for head in range(HEADS):
             product = psum.tile([P, N], F32, name=f"product{head}")

@@ -27,7 +27,7 @@ def tile_bdhhrm_kernel(tc, table, h_init, l_init, w, offs, out):
         offsets = held.tile([P, N // 16], U16, name="offsets")
         nc.sync.dma_start(offsets[:], offs)
         weights = held.tile([D, M], BF16, name="weights")
-        nc.gpsimd.dma_start(weights[:], w)
+        nc.sync.dma_start(weights[:], w)
 
         identity = held.tile([P, P], BF16, name="identity")
         make_identity(nc, identity[:])
@@ -84,15 +84,19 @@ def tile_bdhhrm_kernel(tc, table, h_init, l_init, w, offs, out):
             nc.tensor.transpose(flipped[:], xi_rows[:, b, :], identity[:])
             nc.vector.tensor_copy(xi[:, b * P : (b + 1) * P], flipped[:])
 
-        for head in range(HEADS):
-            product = psum.tile([P, N], F32, name=f"product{head}")
-            nc.tensor.matmul(
-                product[:],
-                weights[:, head * P : (head + 1) * P],
-                xi[:].indirect(offsets[:]),
-                start=True,
-                stop=True,
-            )
-            result = held.tile([P, N], F32, name=f"result{head}")
+        PAIR = 2
+        out_pairs = out.rearrange("(pair head p) j -> pair p head j", head=PAIR, p=P)
+        for pair in range(HEADS // PAIR):
+            product = psum.tile([P, PAIR, N], F32, name=f"product{pair}")
+            for head in range(PAIR):
+                first = (pair * PAIR + head) * P
+                nc.tensor.matmul(
+                    product[:, head, :],
+                    weights[:, first : first + P],
+                    xi[:].indirect(offsets[:]),
+                    start=True,
+                    stop=True,
+                )
+            result = held.tile([P, PAIR, N], F32, name=f"result{pair}")
             nc.vector.tensor_scalar_max(result[:], product[:], 0.0)
-            nc.sync.dma_start(out[head * P : (head + 1) * P, :], result[:])
+            nc.sync.dma_start(out_pairs[pair], result[:])

@@ -38,7 +38,7 @@ def tile_bdhhrm_kernel(tc, table, h_init, l_init, w, offs, out):
         nc.tensor.matmul(states[:], ones[:], state_rows[:], start=True, stop=True)
 
         scratch = psum.tile([P, S], F32, name="scratch")
-        for turn in range(8):
+        for turn in range(6):
             nc.tensor.matmul(
                 scratch[:], words[:, 0, :], words[:].rearrange("p b d -> p (b d)"), start=True, stop=True
             )
@@ -53,26 +53,65 @@ def tile_bdhhrm_kernel(tc, table, h_init, l_init, w, offs, out):
         nc.scalar.activation(
             rstd_a[:], stats_a[:, :, SQUARES], ACT.Abs_reciprocal_sqrt, bias=EPS, scale=1.0 / D
         )
+
+        products = held.tile([P, BLOCKS, D], F32, name="products")
+        joint = [held.tile([P, 1], F32, name=f"joint{b}") for b in range(BLOCKS)]
+
+        def sum_products(b):
+            nc.vector.scalar_tensor_tensor(
+                products[:, b, :], words[:, b, :], stats_a[:, b, MEAN : MEAN + 1], states[:],
+                ALU.subtract, ALU.mult, accum_out=joint[b][:],
+            )
+
+        sum_products(0)
+        stats_c = held.tile([P, 2, 3], F32, name="stats_c")
+        nc.vector.bn_stats(
+            stats_c[:].rearrange("p b k -> p (b k)"), states[:].unsqueeze(2).to_broadcast([P, D, 2])
+        )
+        sum_products(1)
         summed = held.tile([P, BLOCKS, D], F32, name="summed")
         for b in range(BLOCKS):
             nc.vector.scalar_tensor_tensor(
                 summed[:, b, :], words[:, b, :], rstd_a[:, b : b + 1], states[:], ALU.mult, ALU.add
             )
-
-        stats_x = held.tile([P, BLOCKS, 3], F32, name="stats_x")
-        nc.vector.bn_stats(
-            stats_x[:].rearrange("p b k -> p (b k)"), summed[:].rearrange("p b d -> p d b")
-        )
-        rstd_x = held.tile([P, BLOCKS], F32, name="rstd_x")
+        mean_x = held.tile([P, BLOCKS], F32, name="mean_x")
+        for b in range(BLOCKS):
+            nc.vector.tensor_scalar(
+                mean_x[:, b : b + 1], stats_a[:, b, MEAN : MEAN + 1], rstd_a[:, b : b + 1],
+                stats_c[:, 0, MEAN : MEAN + 1], ALU.mult, ALU.add,
+            )
+        rstd_share = held.tile([P, BLOCKS], F32, name="rstd_share")
         nc.scalar.activation(
-            rstd_x[:], stats_x[:, :, SQUARES], ACT.Abs_reciprocal_sqrt, bias=EPS, scale=1.0 / D
+            rstd_share[:], stats_a[:, :, SQUARES], ACT.Abs_reciprocal_sqrt,
+            bias=EPS * (D / 2) ** 2, scale=(D / 2) ** 2 / D,
         )
+        rstd_squared = held.tile([P, BLOCKS], F32, name="rstd_squared")
+        nc.scalar.activation(rstd_squared[:], rstd_a[:], ACT.Square, scale=D ** -0.5)
+        var_t = held.tile([P, BLOCKS], F32, name="var_t")
+        var_both = held.tile([P, BLOCKS], F32, name="var_both")
+        rstd_x = held.tile([P, BLOCKS], F32, name="rstd_x")
+        for b in range(BLOCKS):
+            nc.scalar.activation(
+                var_t[:, b : b + 1], rstd_squared[:, b : b + 1], ACT.Identity,
+                bias=EPS, scale=stats_a[:, b, SQUARES : SQUARES + 1],
+            )
+        for b in range(BLOCKS):
+            nc.scalar.activation(
+                var_both[:, b : b + 1], stats_c[:, 0, SQUARES : SQUARES + 1], ACT.Identity,
+                bias=var_t[:, b : b + 1], scale=1.0 / D,
+            )
+        for b in range(BLOCKS):
+            nc.scalar.activation(
+                rstd_x[:, b : b + 1], joint[b][:], ACT.Abs_reciprocal_sqrt,
+                bias=var_both[:, b : b + 1], scale=rstd_share[:, b : b + 1],
+            )
+
         xi_rows = held.tile([P, BLOCKS, D], BF16, name="xi_rows")
         for b in range(BLOCKS):
             nc.vector.tensor_scalar(
                 xi_rows[:, b, :],
                 summed[:, b, :],
-                stats_x[:, b, MEAN : MEAN + 1],
+                mean_x[:, b : b + 1],
                 rstd_x[:, b : b + 1],
                 ALU.subtract,
                 ALU.mult,

@@ -54,56 +54,48 @@ def tile_bdhhrm_kernel(tc, table, h_init, l_init, w, offs, out):
             rstd_a[:], stats_a[:, :, SQUARES], ACT.Abs_reciprocal_sqrt, bias=EPS, scale=1.0 / D
         )
 
+        half = held.tile([P, BLOCKS], F32, name="half")
+        nc.vector.tensor_scalar(
+            half[:], stats_a[:, :, SQUARES], (1.0 + EPS) / 2, EPS * EPS * D / 2, ALU.mult, ALU.add
+        )
+        share = held.tile([P, BLOCKS], F32, name="share")
+        nc.scalar.activation(
+            share[:], stats_a[:, :, SQUARES], ACT.Abs_reciprocal_sqrt,
+            bias=EPS * (D / 2) ** 2, scale=(D / 2) ** 2 / D,
+        )
         products = held.tile([P, BLOCKS, D], F32, name="products")
         joint = [held.tile([P, 1], F32, name=f"joint{b}") for b in range(BLOCKS)]
-
-        def sum_products(b):
+        for b in range(BLOCKS):
             nc.vector.scalar_tensor_tensor(
                 products[:, b, :], words[:, b, :], stats_a[:, b, MEAN : MEAN + 1], states[:],
                 ALU.subtract, ALU.mult, accum_out=joint[b][:],
             )
-
-        sum_products(0)
-        stats_c = held.tile([P, 2, 3], F32, name="stats_c")
-        nc.vector.bn_stats(
-            stats_c[:].rearrange("p b k -> p (b k)"), states[:].unsqueeze(2).to_broadcast([P, D, 2])
-        )
-        sum_products(1)
+        halves_c = held.tile([P, 6], F32, name="halves_c")
+        nc.vector.bn_stats(halves_c[:], states[:])
+        stats_c = held.tile([P, 2], F32, name="stats_c")
+        nc.vector.bn_aggr(stats_c[:], halves_c[:])
         summed = held.tile([P, BLOCKS, D], F32, name="summed")
         for b in range(BLOCKS):
             nc.vector.scalar_tensor_tensor(
                 summed[:, b, :], words[:, b, :], rstd_a[:, b : b + 1], states[:], ALU.mult, ALU.add
             )
+        inner = held.tile([P, BLOCKS], F32, name="inner")
+        rstd_x = held.tile([P, BLOCKS], F32, name="rstd_x")
         mean_x = held.tile([P, BLOCKS], F32, name="mean_x")
         for b in range(BLOCKS):
-            nc.vector.tensor_scalar(
-                mean_x[:, b : b + 1], stats_a[:, b, MEAN : MEAN + 1], rstd_a[:, b : b + 1],
-                stats_c[:, 0, MEAN : MEAN + 1], ALU.mult, ALU.add,
-            )
-        rstd_share = held.tile([P, BLOCKS], F32, name="rstd_share")
-        nc.scalar.activation(
-            rstd_share[:], stats_a[:, :, SQUARES], ACT.Abs_reciprocal_sqrt,
-            bias=EPS * (D / 2) ** 2, scale=(D / 2) ** 2 / D,
-        )
-        rstd_squared = held.tile([P, BLOCKS], F32, name="rstd_squared")
-        nc.scalar.activation(rstd_squared[:], rstd_a[:], ACT.Square, scale=D ** -0.5)
-        var_t = held.tile([P, BLOCKS], F32, name="var_t")
-        var_both = held.tile([P, BLOCKS], F32, name="var_both")
-        rstd_x = held.tile([P, BLOCKS], F32, name="rstd_x")
-        for b in range(BLOCKS):
             nc.scalar.activation(
-                var_t[:, b : b + 1], rstd_squared[:, b : b + 1], ACT.Identity,
-                bias=EPS, scale=stats_a[:, b, SQUARES : SQUARES + 1],
+                inner[:, b : b + 1], half[:, b : b + 1], ACT.Identity,
+                bias=joint[b][:], scale=rstd_a[:, b : b + 1],
             )
         for b in range(BLOCKS):
             nc.scalar.activation(
-                var_both[:, b : b + 1], stats_c[:, 0, SQUARES : SQUARES + 1], ACT.Identity,
-                bias=var_t[:, b : b + 1], scale=1.0 / D,
+                rstd_x[:, b : b + 1], inner[:, b : b + 1], ACT.Abs_reciprocal_sqrt,
+                bias=stats_c[:, 1:2], scale=share[:, b : b + 1],
             )
         for b in range(BLOCKS):
             nc.scalar.activation(
-                rstd_x[:, b : b + 1], joint[b][:], ACT.Abs_reciprocal_sqrt,
-                bias=var_both[:, b : b + 1], scale=rstd_share[:, b : b + 1],
+                mean_x[:, b : b + 1], stats_a[:, b, MEAN : MEAN + 1], ACT.Identity,
+                bias=stats_c[:, 0:1], scale=rstd_a[:, b : b + 1],
             )
 
         xi_rows = held.tile([P, BLOCKS, D], BF16, name="xi_rows")

@@ -116,14 +116,14 @@ def tile_bdhhrm_kernel(tc, table, h_init, l_init, w, offs, out):
             nc.vector.tensor_copy(xi[:, b * P : (b + 1) * P], flipped[:])
 
         PAIR = 2
-        out_pairs = out.rearrange("(pair head p) j -> pair p head j", head=PAIR, p=P)
+        weight_columns = weights[:].rearrange("d (pair p odd) -> d pair odd p", p=P, odd=PAIR)
+        out_pairs = out.rearrange("(pair p odd) j -> pair p odd j", p=P, odd=PAIR)
         for pair in range(HEADS // PAIR):
             product = psum.tile([P, PAIR, N], F32, name=f"product{pair}")
-            for head in range(PAIR):
-                first = (pair * PAIR + head) * P
+            for odd in range(PAIR):
                 nc.tensor.matmul(
-                    product[:, head, :],
-                    weights[:, first : first + P],
+                    product[:, odd, :],
+                    weight_columns[:, pair, odd, :],
                     xi[:].indirect(offsets[:]),
                     start=True,
                     stop=True,

import concourse.mybir as mybir
from concourse.masks import make_identity

S, D, M, N = 256, 128, 512, 64
P = 128
BLOCKS = S // P
HEADS = M // P
EPS = 1e-5
FLOPS = 2 * D * M * N

BF16, F32, U16 = mybir.dt.bfloat16, mybir.dt.float32, mybir.dt.uint16
ALU = mybir.AluOpType
ACT = mybir.ActivationFunctionType


def tile_bdhhrm_kernel(tc, table, h_init, l_init, w, offs, out):
    nc = tc.nc
    with (
        tc.tile_pool(name="held", bufs=1) as held,
        tc.psum_pool(name="psum", bufs=1) as psum,
    ):
        state_rows = held.tile([2, D], F32, name="state_rows")
        nc.sync.dma_start(state_rows[0:1, :], h_init.rearrange("d one -> one d"))
        nc.scalar.dma_start(state_rows[1:2, :], l_init.rearrange("d one -> one d"))
        words = held.tile([P, BLOCKS, D], BF16, name="words")
        nc.sync.dma_start(words[:], table.rearrange("(b p) d -> p b d", p=P))
        offsets = held.tile([P, N // 16], U16, name="offsets")
        nc.sync.dma_start(offsets[:], offs)
        weights = held.tile([D, M], BF16, name="weights")
        nc.sync.dma_start(weights[:], w)

        identity = held.tile([P, P], BF16, name="identity")
        make_identity(nc, identity[:])

        ones = held.tile([2, P], F32, name="ones")
        nc.vector.memset(ones[:], 1.0)
        states = psum.tile([P, D], F32, name="states")
        nc.tensor.matmul(states[:], ones[:], state_rows[:], start=True, stop=True)

        scratch = psum.tile([P, S], F32, name="scratch")
        for turn in range(6):
            nc.tensor.matmul(
                scratch[:], words[:, 0, :], words[:].rearrange("p b d -> p (b d)"), start=True, stop=True
            )

        MEAN, SQUARES = 1, 2

        stats_a = held.tile([P, BLOCKS, 3], F32, name="stats_a")
        nc.vector.bn_stats(
            stats_a[:].rearrange("p b k -> p (b k)"), words[:].rearrange("p b d -> p d b")
        )
        rstd_a = held.tile([P, BLOCKS], F32, name="rstd_a")
        nc.scalar.activation(
            rstd_a[:], stats_a[:, :, SQUARES], ACT.Abs_reciprocal_sqrt, bias=EPS, scale=1.0 / D
        )

        half = held.tile([P, BLOCKS], F32, name="half")
        nc.vector.tensor_scalar(
            half[:], stats_a[:, :, SQUARES], (1.0 + EPS) / 2, EPS * EPS * D / 2, ALU.mult, ALU.add
        )
        share = held.tile([P, BLOCKS], F32, name="share")
        nc.scalar.activation(
            share[:], stats_a[:, :, SQUARES], ACT.Abs_reciprocal_sqrt,
            bias=EPS * (D / 2) ** 2, scale=(D / 2) ** 2 / D,
        )
        products = held.tile([P, BLOCKS, D], F32, name="products")
        joint = [held.tile([P, 1], F32, name=f"joint{b}") for b in range(BLOCKS)]
        for b in range(BLOCKS):
            nc.vector.scalar_tensor_tensor(
                products[:, b, :], words[:, b, :], stats_a[:, b, MEAN : MEAN + 1], states[:],
                ALU.subtract, ALU.mult, accum_out=joint[b][:],
            )
        halves_c = held.tile([P, 6], F32, name="halves_c")
        nc.vector.bn_stats(halves_c[:], states[:])
        stats_c = held.tile([P, 2], F32, name="stats_c")
        nc.vector.bn_aggr(stats_c[:], halves_c[:])
        summed = held.tile([P, BLOCKS, D], F32, name="summed")
        for b in range(BLOCKS):
            nc.vector.scalar_tensor_tensor(
                summed[:, b, :], words[:, b, :], rstd_a[:, b : b + 1], states[:], ALU.mult, ALU.add
            )
        inner = held.tile([P, BLOCKS], F32, name="inner")
        rstd_x = held.tile([P, BLOCKS], F32, name="rstd_x")
        mean_x = held.tile([P, BLOCKS], F32, name="mean_x")
        for b in range(BLOCKS):
            nc.scalar.activation(
                inner[:, b : b + 1], half[:, b : b + 1], ACT.Identity,
                bias=joint[b][:], scale=rstd_a[:, b : b + 1],
            )
        for b in range(BLOCKS):
            nc.scalar.activation(
                rstd_x[:, b : b + 1], inner[:, b : b + 1], ACT.Abs_reciprocal_sqrt,
                bias=stats_c[:, 1:2], scale=share[:, b : b + 1],
            )
        for b in range(BLOCKS):
            nc.scalar.activation(
                mean_x[:, b : b + 1], stats_a[:, b, MEAN : MEAN + 1], ACT.Identity,
                bias=stats_c[:, 0:1], scale=rstd_a[:, b : b + 1],
            )

        xi_rows = held.tile([P, BLOCKS, D], BF16, name="xi_rows")
        for b in range(BLOCKS):
            nc.vector.tensor_scalar(
                xi_rows[:, b, :],
                summed[:, b, :],
                mean_x[:, b : b + 1],
                rstd_x[:, b : b + 1],
                ALU.subtract,
                ALU.mult,
            )

        xi = held.tile([D, S], BF16, name="xi")
        for b in range(BLOCKS):
            flipped = psum.tile([D, P], BF16, name=f"flipped{b}")
            nc.tensor.transpose(flipped[:], xi_rows[:, b, :], identity[:])
            nc.vector.tensor_copy(xi[:, b * P : (b + 1) * P], flipped[:])

        PAIR = 2
        weight_columns = weights[:].rearrange("d (pair p odd) -> d pair odd p", p=P, odd=PAIR)
        out_pairs = out.rearrange("(pair p odd) j -> pair p odd j", p=P, odd=PAIR)
        for pair in range(HEADS // PAIR):
            product = psum.tile([P, PAIR, N], F32, name=f"product{pair}")
            for odd in range(PAIR):
                nc.tensor.matmul(
                    product[:, odd, :],
                    weight_columns[:, pair, odd, :],
                    xi[:].indirect(offsets[:]),
                    start=True,
                    stop=True,
                )
            result = held.tile([P, PAIR, N], F32, name=f"result{pair}")
            nc.vector.tensor_scalar_max(result[:], product[:], 0.0)
            nc.sync.dma_start(out_pairs[pair], result[:])
